import numpy as np
import ml_dtypes


def mxq(x, axis, fmt="e4m3"):
    dtype, down = {"e4m3": (ml_dtypes.float8_e4m3fn, 7), "e5m2": (ml_dtypes.float8_e5m2, 14)}[fmt]
    v = np.moveaxis(np.asarray(x, np.float32).astype(ml_dtypes.bfloat16).astype(np.float64), axis, -1)
    blocks = v.reshape(v.shape[:-1] + (-1, 32))
    amax = np.abs(blocks).max(-1, keepdims=True)
    byte = np.maximum(np.where(amax > 0, np.frexp(amax)[1] - 1 + 127, 0) - down, 1)
    scale = np.exp2(byte - 127.0)
    codes = (blocks / scale).astype(np.float32).astype(dtype).astype(np.float64)
    return np.moveaxis((codes * scale).reshape(v.shape), -1, axis)


WIDE = False


def mx_kscale(k):
    if not WIDE:
        return np.ones(k)
    levels = np.array([10, -10, 5, -5, 0])
    a = np.random.permutation(np.resize(levels, k // 512 * 4)).reshape(k // 512, 4)
    idx = np.arange(k)
    return np.exp2(a[idx // 512, idx % 128 // 32])


BF16 = ml_dtypes.bfloat16


def bf(x):
    return np.asarray(x, np.float32).astype(BF16)


def f64(x):
    return np.asarray(x).astype(np.float64)


B, CIN, COUT, T, R, C = 2, 512, 512, 4, 4, 4


def setup_inputs():
    s = mx_kscale(CIN)
    x = np.random.standard_normal((B, CIN, T, R, C)) * s[None, :, None, None, None]
    W = np.random.standard_normal((7 * COUT, CIN)) * 0.5 / np.sqrt(CIN) / s[None, :]
    return {"x": bf(x), "W": bf(W)}


def _shift(a, axis, d):
    pads = [(0, 0)] * a.ndim
    idx = [slice(None)] * a.ndim
    if d > 0:
        pads[axis] = (1, 0)
        idx[axis] = slice(0, -1)
    else:
        pads[axis] = (0, 1)
        idx[axis] = slice(1, None)
    return np.pad(a, pads)[tuple(idx)]


def reference(x, W):
    cout = W.shape[0] // 7
    xq = mxq(f64(x), 1, "e4m3")
    Wq = mxq(f64(W), 1, "e4m3")
    all_out = xq.transpose(0, 2, 3, 4, 1) @ Wq.T
    a = all_out.reshape(*all_out.shape[:4], 7, cout)
    out = a[..., 0, :]
    out = out + _shift(a[..., 1, :], 1, +1)
    out = out + _shift(a[..., 2, :], 1, -1)
    out = out + _shift(a[..., 3, :], 2, +1)
    out = out + _shift(a[..., 4, :], 2, -1)
    out = out + _shift(a[..., 5, :], 3, +1)
    out = out + _shift(a[..., 6, :], 3, -1)
    return np.transpose(out, (0, 4, 1, 2, 3))

@@ -1,0 +1,132 @@
+from contextlib import ExitStack
+
+import concourse.masks as masks
+import concourse.mybir as mybir
+
+BF16 = mybir.dt.bfloat16
+F32 = mybir.dt.float32
+U32 = mybir.dt.uint32
+U8 = mybir.dt.uint8
+FP8X4 = mybir.dt.float8_e4m3fn_x4
+
+P = 128
+LANES = 4
+BATCH = 2
+CHANNELS_IN = 512
+CHANNELS_OUT = 512
+SIDE = 4
+VOXELS = SIDE * SIDE * SIDE
+TOKENS = BATCH * VOXELS
+DIRECTIONS = 7
+OUT_TILES = CHANNELS_OUT // P
+HALVES = 2
+TILES_PER_BANK = 2
+BANKS_PER_DIRECTION = OUT_TILES // TILES_PER_BANK
+
+FLOPS = 2 * TOKENS * CHANNELS_IN * DIRECTIONS * CHANNELS_OUT
+
+
+def tile_stackeddirectionalconv3d_s_kernel(tc, x, W, out):
+    nc = tc.nc
+    with ExitStack() as ctx:
+        keep = ctx.enter_context(tc.tile_pool(name="keep", bufs=1))
+        w_pool = ctx.enter_context(tc.tile_pool(name="w_pool", bufs=DIRECTIONS))
+        acc_pool = ctx.enter_context(tc.psum_pool(name="acc_pool", bufs=1))
+        bank_pool = ctx.enter_context(tc.psum_pool(name="bank_pool", bufs=2 * BANKS_PER_DIRECTION))
+        ctx.enter_context(tc.manual_schedule())
+
+        x_raw = keep.tile([P, BATCH * LANES * VOXELS], BF16)
+        nc.sync.dma_start(
+            out=x_raw[:].rearrange("q (g w) -> q g w", g=BATCH * HALVES),
+            in_=x.rearrange("b (u q e) t r c -> (b u) q (e t r c)", u=HALVES, q=P).rearrange("g q w -> q g w"),
+        )
+        w_rows = W.rearrange("(d p j) k -> d p (j k)", d=DIRECTIONS, p=P)
+        w_raw = []
+        for d in range(DIRECTIONS):
+            w_raw_d = w_pool.tile([P, OUT_TILES * CHANNELS_IN], BF16, name="w_raw")
+            nc.sync.dma_start(out=w_raw_d[:], in_=w_rows[d])
+            w_raw.append(w_raw_d)
+
+        identity = keep.tile([P, P], F32)
+        masks.make_identity(nc, identity[:])
+
+        x_moved = keep.tile([P, DIRECTIONS, TOKENS * LANES], BF16, align_bytes=64)
+        x_codes = keep.tile([P, DIRECTIONS, TOKENS], U32, align_bytes=64)
+        x_scales = keep.tile([P, DIRECTIONS, TOKENS], U8, align_bytes=64)
+        nc.vector.memset(x_moved[:, 1:, :], 0.0)
+        nc.vector.tensor_copy(
+            out=x_moved[:, 0, :].rearrange("q (b v i) -> q b v i", b=BATCH, i=LANES),
+            in_=x_raw[:].rearrange("q (b i v) -> q b v i", b=BATCH, i=LANES),
+        )
+        for d in range(1, DIRECTIONS):
+            axis = (d - 1) // 2
+            step = SIDE ** (2 - axis) * LANES
+            period = SIDE * step
+            target = x_moved[:, d, :].rearrange("q (o w) -> q o w", w=period)
+            source = x_moved[:, 0, :].rearrange("q (o w) -> q o w", w=period)
+            if d % 2 == 1:
+                nc.vector.tensor_copy(out=target[:, :, step:], in_=source[:, :, : period - step])
+            else:
+                nc.vector.tensor_copy(out=target[:, :, : period - step], in_=source[:, :, step:])
+        for d in range(DIRECTIONS):
+            nc.vector.quantize_mx(
+                out=x_codes[:, d, :].bitcast(FP8X4), scales=x_scales[:, d, :], in_=x_moved[:, d, :]
+            )
+
+        w_codes = keep.tile([P, DIRECTIONS, CHANNELS_OUT], U32, align_bytes=64)
+        w_scales = keep.tile([P, DIRECTIONS, CHANNELS_OUT], U8, align_bytes=64)
+        acc = [acc_pool.tile([P, TOKENS], F32, name="acc%d" % j) for j in range(OUT_TILES)]
+
+        def transpose_and_quantise(d):
+            w_words = w_raw[d][:].bitcast(F32)
+            w_grouped = w_pool.tile([P, CHANNELS_OUT * LANES], BF16, name="w_grouped", align_bytes=64)
+            columns = TILES_PER_BANK * P
+            for h in range(BANKS_PER_DIRECTION):
+                bank = bank_pool.tile([P, HALVES, columns], F32, name="bank")
+                for jj in range(TILES_PER_BANK):
+                    for u in range(HALVES):
+                        first_word = ((h * TILES_PER_BANK + jj) * HALVES + u) * P
+                        nc.tensor.transpose(
+                            bank[:, u, jj * P : (jj + 1) * P], w_words[:, first_word : first_word + P], identity[:]
+                        )
+                nc.scalar.copy(
+                    out=w_grouped[:]
+                    .bitcast(F32)[:, h * columns * HALVES : (h + 1) * columns * HALVES]
+                    .rearrange("q (c u) -> q c u", u=HALVES),
+                    in_=bank[:].rearrange("q u c -> q c u"),
+                )
+                nc.vector.quantize_mx(
+                    out=w_codes[:, d, h * columns : (h + 1) * columns].bitcast(FP8X4),
+                    scales=w_scales[:, d, h * columns : (h + 1) * columns],
+                    in_=w_grouped[:, h * columns * LANES : (h + 1) * columns * LANES],
+                )
+
+        def multiply(d):
+            for j in range(OUT_TILES):
+                nc.tensor.matmul_mx(
+                    out=acc[j][:],
+                    lhsT=w_codes[:, d, j * P : (j + 1) * P].bitcast(FP8X4),
+                    lhsT_scale=w_scales[:, d, j * P : (j + 1) * P],
+                    rhs=x_codes[:, d, :].bitcast(FP8X4),
+                    rhs_scale=x_scales[:, d, :],
+                    start=(d == 0),
+                    stop=(d == DIRECTIONS - 1),
+                )
+
+        transpose_and_quantise(0)
+        for d in range(1, DIRECTIONS):
+            transpose_and_quantise(d)
+            multiply(d - 1)
+        multiply(DIRECTIONS - 1)
+
+        result = keep.tile([P, BATCH, OUT_TILES, VOXELS], F32)
+        for j in range(OUT_TILES):
+            sums = acc[j][:].rearrange("p (b v) -> p b v", b=BATCH)
+            if j % 2 == 0:
+                nc.scalar.copy(out=result[:, :, j, :], in_=sums)
+            else:
+                nc.vector.tensor_copy(out=result[:, :, j, :], in_=sums)
+        nc.sync.dma_start(
+            out=out.rearrange("b (p j) t r c -> p b (j t r c)", j=OUT_TILES),
+            in_=result[:].rearrange("p b j v -> p b (j v)"),
+        )

@@ -22,6 +22,8 @@ OUT_TILES = CHANNELS_OUT // P
 HALVES = 2
 TILES_PER_BANK = 2
 BANKS_PER_DIRECTION = OUT_TILES // TILES_PER_BANK
+BANK_COLUMNS = 512
+WARMUP_PASSES = 6
 
 FLOPS = 2 * TOKENS * CHANNELS_IN * DIRECTIONS * CHANNELS_OUT
 
@@ -49,6 +51,23 @@ def tile_stackeddirectionalconv3d_s_kernel(tc, x, W, out):
 
         identity = keep.tile([P, P], F32)
         masks.make_identity(nc, identity[:])
+
+        zeros = keep.tile([P, BANK_COLUMNS * LANES], BF16, align_bytes=64)
+        zero_codes = keep.tile([P, BANK_COLUMNS], U32, align_bytes=64)
+        zero_scales = keep.tile([P, BANK_COLUMNS], U8, align_bytes=64)
+        nc.vector.memset(zeros[:], 0.0)
+        nc.vector.quantize_mx(out=zero_codes[:].bitcast(FP8X4), scales=zero_scales[:], in_=zeros[:])
+        unread = bank_pool.tile([P, BANK_COLUMNS], F32, name="bank")
+        for n in range(WARMUP_PASSES):
+            nc.tensor.matmul_mx(
+                out=unread[:],
+                lhsT=zero_codes[:, :P].bitcast(FP8X4),
+                lhsT_scale=zero_scales[:, :P],
+                rhs=zero_codes[:].bitcast(FP8X4),
+                rhs_scale=zero_scales[:],
+                start=True,
+                stop=True,
+            )
 
         x_moved = keep.tile([P, DIRECTIONS, TOKENS * LANES], BF16, align_bytes=64)
         x_codes = keep.tile([P, DIRECTIONS, TOKENS], U32, align_bytes=64)

@@ -7,6 +7,7 @@ BF16 = mybir.dt.bfloat16
 F32 = mybir.dt.float32
 U32 = mybir.dt.uint32
 U8 = mybir.dt.uint8
+I32 = mybir.dt.int32
 FP8X4 = mybir.dt.float8_e4m3fn_x4
 
 P = 128
@@ -22,8 +23,9 @@ OUT_TILES = CHANNELS_OUT // P
 HALVES = 2
 TILES_PER_BANK = 2
 BANKS_PER_DIRECTION = OUT_TILES // TILES_PER_BANK
-BANK_COLUMNS = 512
-WARMUP_PASSES = 6
+RUN = 2
+VECTOR_EVERY = 4
+assert (DIRECTIONS - 1) % RUN == 0
 
 FLOPS = 2 * TOKENS * CHANNELS_IN * DIRECTIONS * CHANNELS_OUT
 
@@ -46,33 +48,22 @@ def tile_stackeddirectionalconv3d_s_kernel(tc, x, W, out):
         w_raw = []
         for d in range(DIRECTIONS):
             w_raw_d = w_pool.tile([P, OUT_TILES * CHANNELS_IN], BF16, name="w_raw")
-            nc.sync.dma_start(out=w_raw_d[:], in_=w_rows[d])
+            pieces = BANKS_PER_DIRECTION if d == DIRECTIONS - 1 else 1
+            width = OUT_TILES * CHANNELS_IN // pieces
+            for piece in range(pieces):
+                nc.sync.dma_start(
+                    out=w_raw_d[:, piece * width : (piece + 1) * width],
+                    in_=w_rows[d, :, piece * width : (piece + 1) * width],
+                )
             w_raw.append(w_raw_d)
 
         identity = keep.tile([P, P], F32)
         masks.make_identity(nc, identity[:])
 
-        zeros = keep.tile([P, BANK_COLUMNS * LANES], BF16, align_bytes=64)
-        zero_codes = keep.tile([P, BANK_COLUMNS], U32, align_bytes=64)
-        zero_scales = keep.tile([P, BANK_COLUMNS], U8, align_bytes=64)
-        nc.vector.memset(zeros[:], 0.0)
-        nc.vector.quantize_mx(out=zero_codes[:].bitcast(FP8X4), scales=zero_scales[:], in_=zeros[:])
-        unread = bank_pool.tile([P, BANK_COLUMNS], F32, name="bank")
-        for n in range(WARMUP_PASSES):
-            nc.tensor.matmul_mx(
-                out=unread[:],
-                lhsT=zero_codes[:, :P].bitcast(FP8X4),
-                lhsT_scale=zero_scales[:, :P],
-                rhs=zero_codes[:].bitcast(FP8X4),
-                rhs_scale=zero_scales[:],
-                start=True,
-                stop=True,
-            )
-
         x_moved = keep.tile([P, DIRECTIONS, TOKENS * LANES], BF16, align_bytes=64)
         x_codes = keep.tile([P, DIRECTIONS, TOKENS], U32, align_bytes=64)
         x_scales = keep.tile([P, DIRECTIONS, TOKENS], U8, align_bytes=64)
-        nc.vector.memset(x_moved[:, 1:, :], 0.0)
+        nc.vector.memset(x_moved[:, 1:, :].bitcast(I32), 0)
         nc.vector.tensor_copy(
             out=x_moved[:, 0, :].rearrange("q (b v i) -> q b v i", b=BATCH, i=LANES),
             in_=x_raw[:].rearrange("q (b i v) -> q b v i", b=BATCH, i=LANES),
@@ -108,12 +99,16 @@ def tile_stackeddirectionalconv3d_s_kernel(tc, x, W, out):
                         nc.tensor.transpose(
                             bank[:, u, jj * P : (jj + 1) * P], w_words[:, first_word : first_word + P], identity[:]
                         )
-                nc.scalar.copy(
-                    out=w_grouped[:]
+                side_by_side = (
+                    w_grouped[:]
                     .bitcast(F32)[:, h * columns * HALVES : (h + 1) * columns * HALVES]
-                    .rearrange("q (c u) -> q c u", u=HALVES),
-                    in_=bank[:].rearrange("q u c -> q c u"),
+                    .rearrange("q (c u) -> q c u", u=HALVES)
                 )
+                if (d * BANKS_PER_DIRECTION + h) % VECTOR_EVERY == VECTOR_EVERY - 1:
+                    nc.vector.tensor_copy(out=side_by_side, in_=bank[:].rearrange("q u c -> q c u"))
+                else:
+                    nc.scalar.copy(out=side_by_side, in_=bank[:].rearrange("q u c -> q c u"))
+            for h in range(BANKS_PER_DIRECTION):
                 nc.vector.quantize_mx(
                     out=w_codes[:, d, h * columns : (h + 1) * columns].bitcast(FP8X4),
                     scales=w_scales[:, d, h * columns : (h + 1) * columns],
@@ -133,19 +128,25 @@ def tile_stackeddirectionalconv3d_s_kernel(tc, x, W, out):
                 )
 
         transpose_and_quantise(0)
-        for d in range(1, DIRECTIONS):
-            transpose_and_quantise(d)
-            multiply(d - 1)
-        multiply(DIRECTIONS - 1)
+        for first in range(1, DIRECTIONS, RUN):
+            for d in range(first, first + RUN):
+                transpose_and_quantise(d)
+            for d in range(max(first - RUN, 0), first):
+                multiply(d)
+        for d in range(DIRECTIONS - RUN, DIRECTIONS):
+            multiply(d)
 
         result = keep.tile([P, BATCH, OUT_TILES, VOXELS], F32)
-        for j in range(OUT_TILES):
-            sums = acc[j][:].rearrange("p (b v) -> p b v", b=BATCH)
-            if j % 2 == 0:
-                nc.scalar.copy(out=result[:, :, j, :], in_=sums)
-            else:
-                nc.vector.tensor_copy(out=result[:, :, j, :], in_=sums)
-        nc.sync.dma_start(
-            out=out.rearrange("b (p j) t r c -> p b (j t r c)", j=OUT_TILES),
-            in_=result[:].rearrange("p b j v -> p b (j v)"),
-        )
+        out_rows = out.rearrange("b (p j) t r c -> p b j (t r c)", j=OUT_TILES)
+        for h in range(BANKS_PER_DIRECTION):
+            first_tile = h * TILES_PER_BANK
+            for j in range(first_tile, first_tile + TILES_PER_BANK):
+                sums = acc[j][:].rearrange("p (b v) -> p b v", b=BATCH)
+                if j % 2 == 0:
+                    nc.scalar.copy(out=result[:, :, j, :], in_=sums)
+                else:
+                    nc.vector.tensor_copy(out=result[:, :, j, :], in_=sums)
+            nc.sync.dma_start(
+                out=out_rows[:, :, first_tile : first_tile + TILES_PER_BANK, :],
+                in_=result[:, :, first_tile : first_tile + TILES_PER_BANK, :],
+            )

@@ -21,8 +21,8 @@ TOKENS = BATCH * VOXELS
 DIRECTIONS = 7
 OUT_TILES = CHANNELS_OUT // P
 HALVES = 2
-TILES_PER_BANK = 2
-BANKS_PER_DIRECTION = OUT_TILES // TILES_PER_BANK
+EVEN_PIECES = ((0, 2), (2, 2))
+TAPERED_PIECES = ((0, 2), (2, 1), (3, 1))
 RUN = 2
 VECTOR_EVERY = 4
 assert (DIRECTIONS - 1) % RUN == 0
@@ -36,7 +36,7 @@ def tile_stackeddirectionalconv3d_s_kernel(tc, x, W, out):
         keep = ctx.enter_context(tc.tile_pool(name="keep", bufs=1))
         w_pool = ctx.enter_context(tc.tile_pool(name="w_pool", bufs=DIRECTIONS))
         acc_pool = ctx.enter_context(tc.psum_pool(name="acc_pool", bufs=1))
-        bank_pool = ctx.enter_context(tc.psum_pool(name="bank_pool", bufs=2 * BANKS_PER_DIRECTION))
+        bank_pool = ctx.enter_context(tc.psum_pool(name="bank_pool", bufs=RUN * len(EVEN_PIECES)))
         ctx.enter_context(tc.manual_schedule())
 
         x_raw = keep.tile([P, BATCH * LANES * VOXELS], BF16)
@@ -48,13 +48,9 @@ def tile_stackeddirectionalconv3d_s_kernel(tc, x, W, out):
         w_raw = []
         for d in range(DIRECTIONS):
             w_raw_d = w_pool.tile([P, OUT_TILES * CHANNELS_IN], BF16, name="w_raw")
-            pieces = BANKS_PER_DIRECTION if d == DIRECTIONS - 1 else 1
-            width = OUT_TILES * CHANNELS_IN // pieces
-            for piece in range(pieces):
-                nc.sync.dma_start(
-                    out=w_raw_d[:, piece * width : (piece + 1) * width],
-                    in_=w_rows[d, :, piece * width : (piece + 1) * width],
-                )
+            for first_tile, tiles in TAPERED_PIECES if d == DIRECTIONS - 1 else ((0, OUT_TILES),):
+                columns = slice(first_tile * CHANNELS_IN, (first_tile + tiles) * CHANNELS_IN)
+                nc.sync.dma_start(out=w_raw_d[:, columns], in_=w_rows[d, :, columns])
             w_raw.append(w_raw_d)
 
         identity = keep.tile([P, P], F32)
@@ -88,31 +84,31 @@ def tile_stackeddirectionalconv3d_s_kernel(tc, x, W, out):
         acc = [acc_pool.tile([P, TOKENS], F32, name="acc%d" % j) for j in range(OUT_TILES)]
 
         def transpose_and_quantise(d):
+            pieces = TAPERED_PIECES if d == DIRECTIONS - 1 else EVEN_PIECES
             w_words = w_raw[d][:].bitcast(F32)
             w_grouped = w_pool.tile([P, CHANNELS_OUT * LANES], BF16, name="w_grouped", align_bytes=64)
-            columns = TILES_PER_BANK * P
-            for h in range(BANKS_PER_DIRECTION):
-                bank = bank_pool.tile([P, HALVES, columns], F32, name="bank")
-                for jj in range(TILES_PER_BANK):
+            w_grouped_words = w_grouped[:].bitcast(F32)
+            for i, (first_tile, tiles) in enumerate(pieces):
+                bank = bank_pool.tile([P, HALVES, tiles * P], F32, name="bank")
+                for jj in range(tiles):
                     for u in range(HALVES):
-                        first_word = ((h * TILES_PER_BANK + jj) * HALVES + u) * P
+                        first_word = ((first_tile + jj) * HALVES + u) * P
                         nc.tensor.transpose(
                             bank[:, u, jj * P : (jj + 1) * P], w_words[:, first_word : first_word + P], identity[:]
                         )
-                side_by_side = (
-                    w_grouped[:]
-                    .bitcast(F32)[:, h * columns * HALVES : (h + 1) * columns * HALVES]
-                    .rearrange("q (c u) -> q c u", u=HALVES)
-                )
-                if (d * BANKS_PER_DIRECTION + h) % VECTOR_EVERY == VECTOR_EVERY - 1:
+                side_by_side = w_grouped_words[
+                    :, first_tile * P * HALVES : (first_tile + tiles) * P * HALVES
+                ].rearrange("q (c u) -> q c u", u=HALVES)
+                if (d * len(EVEN_PIECES) + i) % VECTOR_EVERY == VECTOR_EVERY - 1:
                     nc.vector.tensor_copy(out=side_by_side, in_=bank[:].rearrange("q u c -> q c u"))
                 else:
                     nc.scalar.copy(out=side_by_side, in_=bank[:].rearrange("q u c -> q c u"))
-            for h in range(BANKS_PER_DIRECTION):
+            for first_tile, tiles in pieces:
+                columns = slice(first_tile * P, (first_tile + tiles) * P)
                 nc.vector.quantize_mx(
-                    out=w_codes[:, d, h * columns : (h + 1) * columns].bitcast(FP8X4),
-                    scales=w_scales[:, d, h * columns : (h + 1) * columns],
-                    in_=w_grouped[:, h * columns * LANES : (h + 1) * columns * LANES],
+                    out=w_codes[:, d, columns].bitcast(FP8X4),
+                    scales=w_scales[:, d, columns],
+                    in_=w_grouped[:, first_tile * P * LANES : (first_tile + tiles) * P * LANES],
                 )
 
         def multiply(d):
@@ -138,15 +134,14 @@ def tile_stackeddirectionalconv3d_s_kernel(tc, x, W, out):
 
         result = keep.tile([P, BATCH, OUT_TILES, VOXELS], F32)
         out_rows = out.rearrange("b (p j) t r c -> p b j (t r c)", j=OUT_TILES)
-        for h in range(BANKS_PER_DIRECTION):
-            first_tile = h * TILES_PER_BANK
-            for j in range(first_tile, first_tile + TILES_PER_BANK):
+        for first_tile, tiles in TAPERED_PIECES:
+            for j in range(first_tile, first_tile + tiles):
                 sums = acc[j][:].rearrange("p (b v) -> p b v", b=BATCH)
                 if j % 2 == 0:
                     nc.scalar.copy(out=result[:, :, j, :], in_=sums)
                 else:
                     nc.vector.tensor_copy(out=result[:, :, j, :], in_=sums)
             nc.sync.dma_start(
-                out=out_rows[:, :, first_tile : first_tile + TILES_PER_BANK, :],
-                in_=result[:, :, first_tile : first_tile + TILES_PER_BANK, :],
+                out=out_rows[:, :, first_tile : first_tile + tiles, :],
+                in_=result[:, :, first_tile : first_tile + tiles, :],
             )

@@ -21,9 +21,10 @@ TOKENS = BATCH * VOXELS
 DIRECTIONS = 7
 OUT_TILES = CHANNELS_OUT // P
 HALVES = 2
-EVEN_PIECES = ((0, 2), (2, 2))
-TAPERED_PIECES = ((0, 2), (2, 1), (3, 1))
+TILES_PER_BANK = 2
+BANKS_PER_DIRECTION = OUT_TILES // TILES_PER_BANK
 RUN = 2
+WARMUP_PASSES = 24
 VECTOR_EVERY = 4
 assert (DIRECTIONS - 1) % RUN == 0
 
@@ -36,7 +37,7 @@ def tile_stackeddirectionalconv3d_s_kernel(tc, x, W, out):
         keep = ctx.enter_context(tc.tile_pool(name="keep", bufs=1))
         w_pool = ctx.enter_context(tc.tile_pool(name="w_pool", bufs=DIRECTIONS))
         acc_pool = ctx.enter_context(tc.psum_pool(name="acc_pool", bufs=1))
-        bank_pool = ctx.enter_context(tc.psum_pool(name="bank_pool", bufs=RUN * len(EVEN_PIECES)))
+        bank_pool = ctx.enter_context(tc.psum_pool(name="bank_pool", bufs=2 * BANKS_PER_DIRECTION))
         ctx.enter_context(tc.manual_schedule())
 
         x_raw = keep.tile([P, BATCH * LANES * VOXELS], BF16)
@@ -48,13 +49,23 @@ def tile_stackeddirectionalconv3d_s_kernel(tc, x, W, out):
         w_raw = []
         for d in range(DIRECTIONS):
             w_raw_d = w_pool.tile([P, OUT_TILES * CHANNELS_IN], BF16, name="w_raw")
-            for first_tile, tiles in TAPERED_PIECES if d == DIRECTIONS - 1 else ((0, OUT_TILES),):
-                columns = slice(first_tile * CHANNELS_IN, (first_tile + tiles) * CHANNELS_IN)
-                nc.sync.dma_start(out=w_raw_d[:, columns], in_=w_rows[d, :, columns])
+            pieces = BANKS_PER_DIRECTION if d == DIRECTIONS - 1 else 1
+            width = OUT_TILES * CHANNELS_IN // pieces
+            for piece in range(pieces):
+                nc.sync.dma_start(
+                    out=w_raw_d[:, piece * width : (piece + 1) * width],
+                    in_=w_rows[d, :, piece * width : (piece + 1) * width],
+                )
             w_raw.append(w_raw_d)
 
         identity = keep.tile([P, P], F32)
         masks.make_identity(nc, identity[:])
+
+        zeros = keep.tile([P, P * LANES], BF16, align_bytes=64)
+        zero_codes = keep.tile([P, P], U32, align_bytes=64)
+        zero_scales = keep.tile([P, P], U8, align_bytes=64)
+        nc.vector.memset(zeros[:].bitcast(I32), 0)
+        nc.vector.quantize_mx(out=zero_codes[:].bitcast(FP8X4), scales=zero_scales[:], in_=zeros[:])
 
         x_moved = keep.tile([P, DIRECTIONS, TOKENS * LANES], BF16, align_bytes=64)
         x_codes = keep.tile([P, DIRECTIONS, TOKENS], U32, align_bytes=64)
@@ -84,31 +95,31 @@ def tile_stackeddirectionalconv3d_s_kernel(tc, x, W, out):
         acc = [acc_pool.tile([P, TOKENS], F32, name="acc%d" % j) for j in range(OUT_TILES)]
 
         def transpose_and_quantise(d):
-            pieces = TAPERED_PIECES if d == DIRECTIONS - 1 else EVEN_PIECES
             w_words = w_raw[d][:].bitcast(F32)
             w_grouped = w_pool.tile([P, CHANNELS_OUT * LANES], BF16, name="w_grouped", align_bytes=64)
-            w_grouped_words = w_grouped[:].bitcast(F32)
-            for i, (first_tile, tiles) in enumerate(pieces):
-                bank = bank_pool.tile([P, HALVES, tiles * P], F32, name="bank")
-                for jj in range(tiles):
+            columns = TILES_PER_BANK * P
+            for h in range(BANKS_PER_DIRECTION):
+                bank = bank_pool.tile([P, HALVES, columns], F32, name="bank")
+                for jj in range(TILES_PER_BANK):
                     for u in range(HALVES):
-                        first_word = ((first_tile + jj) * HALVES + u) * P
+                        first_word = ((h * TILES_PER_BANK + jj) * HALVES + u) * P
                         nc.tensor.transpose(
                             bank[:, u, jj * P : (jj + 1) * P], w_words[:, first_word : first_word + P], identity[:]
                         )
-                side_by_side = w_grouped_words[
-                    :, first_tile * P * HALVES : (first_tile + tiles) * P * HALVES
-                ].rearrange("q (c u) -> q c u", u=HALVES)
-                if (d * len(EVEN_PIECES) + i) % VECTOR_EVERY == VECTOR_EVERY - 1:
+                side_by_side = (
+                    w_grouped[:]
+                    .bitcast(F32)[:, h * columns * HALVES : (h + 1) * columns * HALVES]
+                    .rearrange("q (c u) -> q c u", u=HALVES)
+                )
+                if (d * BANKS_PER_DIRECTION + h) % VECTOR_EVERY == VECTOR_EVERY - 1:
                     nc.vector.tensor_copy(out=side_by_side, in_=bank[:].rearrange("q u c -> q c u"))
                 else:
                     nc.scalar.copy(out=side_by_side, in_=bank[:].rearrange("q u c -> q c u"))
-            for first_tile, tiles in pieces:
-                columns = slice(first_tile * P, (first_tile + tiles) * P)
+            for h in range(BANKS_PER_DIRECTION):
                 nc.vector.quantize_mx(
-                    out=w_codes[:, d, columns].bitcast(FP8X4),
-                    scales=w_scales[:, d, columns],
-                    in_=w_grouped[:, first_tile * P * LANES : (first_tile + tiles) * P * LANES],
+                    out=w_codes[:, d, h * columns : (h + 1) * columns].bitcast(FP8X4),
+                    scales=w_scales[:, d, h * columns : (h + 1) * columns],
+                    in_=w_grouped[:, h * columns * LANES : (h + 1) * columns * LANES],
                 )
 
         def multiply(d):
@@ -123,9 +134,24 @@ def tile_stackeddirectionalconv3d_s_kernel(tc, x, W, out):
                     stop=(d == DIRECTIONS - 1),
                 )
 
+        def multiply_zeros(passes):
+            for n in range(passes):
+                nc.tensor.matmul_mx(
+                    out=acc[0][:],
+                    lhsT=zero_codes[:].bitcast(FP8X4),
+                    lhsT_scale=zero_scales[:],
+                    rhs=zero_codes[:].bitcast(FP8X4),
+                    rhs_scale=zero_scales[:],
+                    start=True,
+                    stop=True,
+                )
+
+        multiply_zeros(WARMUP_PASSES)
         transpose_and_quantise(0)
         for first in range(1, DIRECTIONS, RUN):
             for d in range(first, first + RUN):
+                if first == 1:
+                    multiply_zeros(OUT_TILES)
                 transpose_and_quantise(d)
             for d in range(max(first - RUN, 0), first):
                 multiply(d)
@@ -134,14 +160,15 @@ def tile_stackeddirectionalconv3d_s_kernel(tc, x, W, out):
 
         result = keep.tile([P, BATCH, OUT_TILES, VOXELS], F32)
         out_rows = out.rearrange("b (p j) t r c -> p b j (t r c)", j=OUT_TILES)
-        for first_tile, tiles in TAPERED_PIECES:
-            for j in range(first_tile, first_tile + tiles):
+        for h in range(BANKS_PER_DIRECTION):
+            first_tile = h * TILES_PER_BANK
+            for j in range(first_tile, first_tile + TILES_PER_BANK):
                 sums = acc[j][:].rearrange("p (b v) -> p b v", b=BATCH)
                 if j % 2 == 0:
                     nc.scalar.copy(out=result[:, :, j, :], in_=sums)
                 else:
                     nc.vector.tensor_copy(out=result[:, :, j, :], in_=sums)
             nc.sync.dma_start(
-                out=out_rows[:, :, first_tile : first_tile + tiles, :],
-                in_=result[:, :, first_tile : first_tile + tiles, :],
+                out=out_rows[:, :, first_tile : first_tile + TILES_PER_BANK, :],
+                in_=result[:, :, first_tile : first_tile + TILES_PER_BANK, :],
             )

from contextlib import ExitStack

import concourse.masks as masks
import concourse.mybir as mybir

BF16 = mybir.dt.bfloat16
F32 = mybir.dt.float32
U32 = mybir.dt.uint32
U8 = mybir.dt.uint8
I32 = mybir.dt.int32
FP8X4 = mybir.dt.float8_e4m3fn_x4

P = 128
LANES = 4
BATCH = 2
CHANNELS_IN = 512
CHANNELS_OUT = 512
SIDE = 4
VOXELS = SIDE * SIDE * SIDE
TOKENS = BATCH * VOXELS
DIRECTIONS = 7
OUT_TILES = CHANNELS_OUT // P
HALVES = 2
TILES_PER_BANK = 2
BANKS_PER_DIRECTION = OUT_TILES // TILES_PER_BANK
RUN = 2
WARMUP_PASSES = 24
VECTOR_EVERY = 4
assert (DIRECTIONS - 1) % RUN == 0

FLOPS = 2 * TOKENS * CHANNELS_IN * DIRECTIONS * CHANNELS_OUT


def tile_stackeddirectionalconv3d_s_kernel(tc, x, W, out):
    nc = tc.nc
    with ExitStack() as ctx:
        keep = ctx.enter_context(tc.tile_pool(name="keep", bufs=1))
        w_pool = ctx.enter_context(tc.tile_pool(name="w_pool", bufs=DIRECTIONS))
        acc_pool = ctx.enter_context(tc.psum_pool(name="acc_pool", bufs=1))
        bank_pool = ctx.enter_context(tc.psum_pool(name="bank_pool", bufs=2 * BANKS_PER_DIRECTION))
        ctx.enter_context(tc.manual_schedule())

        x_raw = keep.tile([P, BATCH * LANES * VOXELS], BF16)
        nc.sync.dma_start(
            out=x_raw[:].rearrange("q (g w) -> q g w", g=BATCH * HALVES),
            in_=x.rearrange("b (u q e) t r c -> (b u) q (e t r c)", u=HALVES, q=P).rearrange("g q w -> q g w"),
        )
        w_rows = W.rearrange("(d p j) k -> d p (j k)", d=DIRECTIONS, p=P)
        w_raw = []
        for d in range(DIRECTIONS):
            w_raw_d = w_pool.tile([P, OUT_TILES * CHANNELS_IN], BF16, name="w_raw")
            pieces = BANKS_PER_DIRECTION if d == DIRECTIONS - 1 else 1
            width = OUT_TILES * CHANNELS_IN // pieces
            for piece in range(pieces):
                nc.sync.dma_start(
                    out=w_raw_d[:, piece * width : (piece + 1) * width],
                    in_=w_rows[d, :, piece * width : (piece + 1) * width],
                )
            w_raw.append(w_raw_d)

        identity = keep.tile([P, P], F32)
        masks.make_identity(nc, identity[:])

        zeros = keep.tile([P, P * LANES], BF16, align_bytes=64)
        zero_codes = keep.tile([P, P], U32, align_bytes=64)
        zero_scales = keep.tile([P, P], U8, align_bytes=64)
        nc.vector.memset(zeros[:].bitcast(I32), 0)
        nc.vector.quantize_mx(out=zero_codes[:].bitcast(FP8X4), scales=zero_scales[:], in_=zeros[:])

        x_moved = keep.tile([P, DIRECTIONS, TOKENS * LANES], BF16, align_bytes=64)
        x_codes = keep.tile([P, DIRECTIONS, TOKENS], U32, align_bytes=64)
        x_scales = keep.tile([P, DIRECTIONS, TOKENS], U8, align_bytes=64)
        nc.vector.memset(x_moved[:, 1:, :].bitcast(I32), 0)
        nc.vector.tensor_copy(
            out=x_moved[:, 0, :].rearrange("q (b v i) -> q b v i", b=BATCH, i=LANES),
            in_=x_raw[:].rearrange("q (b i v) -> q b v i", b=BATCH, i=LANES),
        )
        for d in range(1, DIRECTIONS):
            axis = (d - 1) // 2
            step = SIDE ** (2 - axis) * LANES
            period = SIDE * step
            target = x_moved[:, d, :].rearrange("q (o w) -> q o w", w=period)
            source = x_moved[:, 0, :].rearrange("q (o w) -> q o w", w=period)
            if d % 2 == 1:
                nc.vector.tensor_copy(out=target[:, :, step:], in_=source[:, :, : period - step])
            else:
                nc.vector.tensor_copy(out=target[:, :, : period - step], in_=source[:, :, step:])
        for d in range(DIRECTIONS):
            nc.vector.quantize_mx(
                out=x_codes[:, d, :].bitcast(FP8X4), scales=x_scales[:, d, :], in_=x_moved[:, d, :]
            )

        w_codes = keep.tile([P, DIRECTIONS, CHANNELS_OUT], U32, align_bytes=64)
        w_scales = keep.tile([P, DIRECTIONS, CHANNELS_OUT], U8, align_bytes=64)
        acc = [acc_pool.tile([P, TOKENS], F32, name="acc%d" % j) for j in range(OUT_TILES)]

        def transpose_and_quantise(d):
            w_words = w_raw[d][:].bitcast(F32)
            w_grouped = w_pool.tile([P, CHANNELS_OUT * LANES], BF16, name="w_grouped", align_bytes=64)
            columns = TILES_PER_BANK * P
            for h in range(BANKS_PER_DIRECTION):
                bank = bank_pool.tile([P, HALVES, columns], F32, name="bank")
                for jj in range(TILES_PER_BANK):
                    for u in range(HALVES):
                        first_word = ((h * TILES_PER_BANK + jj) * HALVES + u) * P
                        nc.tensor.transpose(
                            bank[:, u, jj * P : (jj + 1) * P], w_words[:, first_word : first_word + P], identity[:]
                        )
                side_by_side = (
                    w_grouped[:]
                    .bitcast(F32)[:, h * columns * HALVES : (h + 1) * columns * HALVES]
                    .rearrange("q (c u) -> q c u", u=HALVES)
                )
                if (d * BANKS_PER_DIRECTION + h) % VECTOR_EVERY == VECTOR_EVERY - 1:
                    nc.vector.tensor_copy(out=side_by_side, in_=bank[:].rearrange("q u c -> q c u"))
                else:
                    nc.scalar.copy(out=side_by_side, in_=bank[:].rearrange("q u c -> q c u"))
            for h in range(BANKS_PER_DIRECTION):
                nc.vector.quantize_mx(
                    out=w_codes[:, d, h * columns : (h + 1) * columns].bitcast(FP8X4),
                    scales=w_scales[:, d, h * columns : (h + 1) * columns],
                    in_=w_grouped[:, h * columns * LANES : (h + 1) * columns * LANES],
                )

        def multiply(d):
            for j in range(OUT_TILES):
                nc.tensor.matmul_mx(
                    out=acc[j][:],
                    lhsT=w_codes[:, d, j * P : (j + 1) * P].bitcast(FP8X4),
                    lhsT_scale=w_scales[:, d, j * P : (j + 1) * P],
                    rhs=x_codes[:, d, :].bitcast(FP8X4),
                    rhs_scale=x_scales[:, d, :],
                    start=(d == 0),
                    stop=(d == DIRECTIONS - 1),
                )

        def multiply_zeros(passes):
            for n in range(passes):
                nc.tensor.matmul_mx(
                    out=acc[0][:],
                    lhsT=zero_codes[:].bitcast(FP8X4),
                    lhsT_scale=zero_scales[:],
                    rhs=zero_codes[:].bitcast(FP8X4),
                    rhs_scale=zero_scales[:],
                    start=True,
                    stop=True,
                )

        multiply_zeros(WARMUP_PASSES)
        transpose_and_quantise(0)
        for first in range(1, DIRECTIONS, RUN):
            for d in range(first, first + RUN):
                if first == 1:
                    multiply_zeros(OUT_TILES)
                transpose_and_quantise(d)
            for d in range(max(first - RUN, 0), first):
                multiply(d)
        for d in range(DIRECTIONS - RUN, DIRECTIONS):
            multiply(d)

        result = keep.tile([P, BATCH, OUT_TILES, VOXELS], F32)
        out_rows = out.rearrange("b (p j) t r c -> p b j (t r c)", j=OUT_TILES)
        for h in range(BANKS_PER_DIRECTION):
            first_tile = h * TILES_PER_BANK
            for j in range(first_tile, first_tile + TILES_PER_BANK):
                sums = acc[j][:].rearrange("p (b v) -> p b v", b=BATCH)
                if j % 2 == 0:
                    nc.scalar.copy(out=result[:, :, j, :], in_=sums)
                else:
                    nc.vector.tensor_copy(out=result[:, :, j, :], in_=sums)
            nc.sync.dma_start(
                out=out_rows[:, :, first_tile : first_tile + TILES_PER_BANK, :],
                in_=result[:, :, first_tile : first_tile + TILES_PER_BANK, :],
            )
